import numpy as np
import ml_dtypes


def mxq(x, axis, fmt="e4m3"):
    dtype, down = {"e4m3": (ml_dtypes.float8_e4m3fn, 7), "e5m2": (ml_dtypes.float8_e5m2, 14)}[fmt]
    v = np.moveaxis(np.asarray(x, np.float32).astype(ml_dtypes.bfloat16).astype(np.float64), axis, -1)
    blocks = v.reshape(v.shape[:-1] + (-1, 32))
    amax = np.abs(blocks).max(-1, keepdims=True)
    byte = np.maximum(np.where(amax > 0, np.frexp(amax)[1] - 1 + 127, 0) - down, 1)
    scale = np.exp2(byte - 127.0)
    codes = (blocks / scale).astype(np.float32).astype(dtype).astype(np.float64)
    return np.moveaxis((codes * scale).reshape(v.shape), -1, axis)


WIDE = False


def mx_kscale(k):
    if not WIDE:
        return np.ones(k)
    levels = np.array([10, -10, 5, -5, 0])
    a = np.random.permutation(np.resize(levels, k // 512 * 4)).reshape(k // 512, 4)
    idx = np.arange(k)
    return np.exp2(a[idx // 512, idx % 128 // 32])


BF16 = ml_dtypes.bfloat16


def bf(x):
    return np.asarray(x, np.float32).astype(BF16)


def f64(x):
    return np.asarray(x).astype(np.float64)


B, S, H, D = 2, 2048, 8, 64
E = H * D
HALF = D // 2


def rotate_half(u):
    u1, u2 = np.split(u, 2, axis=-1)
    return np.concatenate([-u2, u1], axis=-1)


def apply_rope(t, sin, cos):
    x1, x2 = np.split(t, 2, axis=-1)
    x_rot = x1 * cos + rotate_half(x1) * sin
    return np.concatenate([x_rot, x2], axis=-1)


def setup_inputs():
    s = mx_kscale(E)
    th = np.random.uniform(0.0, 2.0 * np.pi, (S, HALF))
    return {"x": bf(np.random.standard_normal((B, S, E)) * s),
            "W_qkv": bf(np.random.standard_normal((E, 3 * E)) / np.sqrt(E) / s[:, None]),
            "b_qkv": bf(np.random.standard_normal(3 * E) * 0.2),
            "sin_tab": bf(np.sin(th)),
            "cos_tab": bf(np.cos(th))}


def reference(x, W_qkv, b_qkv, sin_tab, cos_tab):
    qkv = (mxq(f64(x), 2, "e4m3") @ mxq(f64(W_qkv), 0, "e4m3")) + f64(b_qkv)
    q, k, v = np.split(qkv, 3, axis=-1)
    q = q.reshape(B, S, H, D)
    k = k.reshape(B, S, H, D)
    v = v.reshape(B, S, H, D)
    sin = f64(sin_tab)[None, :, None, :]
    cos = f64(cos_tab)[None, :, None, :]
    q_rot = apply_rope(q, sin, cos)
    k_rot = apply_rope(k, sin, cos)
    return q_rot, k_rot, v

@@ -1,0 +1,304 @@
+from contextlib import ExitStack
+
+import concourse.mybir as mybir
+from concourse.masks import make_identity
+
+F32 = mybir.dt.float32
+BF16 = mybir.dt.bfloat16
+U32 = mybir.dt.uint32
+U8 = mybir.dt.uint8
+FP8X4 = mybir.dt.float8_e4m3fn_x4
+ALU = mybir.AluOpType
+
+P = 128
+TOKENS = 4096
+E = 512
+GROUPS = 8
+T = 4
+FLOPS = 2 * TOKENS * E * 3 * E
+
+ROT, PAS, VAL = 0, 512, 1024
+N_ON_VECTOR = (2, 3)
+
+
+def tile_improvedattention_pa_t_kernel(
+    tc, x, W_qkv, b_qkv, sin_tab, cos_tab, out_0, out_1, out_2
+):
+    nc = tc.nc
+    xf = x.flatten_outer_dims()
+    outs = [o.rearrange("b s h d -> (b s) (h d)") for o in (out_0, out_1, out_2)]
+
+    with ExitStack() as ctx:
+        const = ctx.enter_context(tc.tile_pool(name="const", bufs=1))
+        xin = ctx.enter_context(tc.tile_pool(name="xin", bufs=GROUPS))
+        xgr = ctx.enter_context(tc.tile_pool(name="xgr", bufs=2))
+        xq = ctx.enter_context(tc.tile_pool(name="xq", bufs=3))
+        mwp = ctx.enter_context(tc.tile_pool(name="mwp", bufs=2))
+        oqkp = ctx.enter_context(tc.tile_pool(name="oqkp", bufs=3))
+        ovp = ctx.enter_context(tc.tile_pool(name="ovp", bufs=3))
+        psr = ctx.enter_context(tc.psum_pool(name="psr", bufs=2))
+        psa = ctx.enter_context(tc.psum_pool(name="psa", bufs=3))
+        pst = ctx.enter_context(tc.psum_pool(name="pst", bufs=3))
+        ctx.enter_context(nc.allow_non_contiguous_dma(reason="short rows of tables and column chunks"))
+
+        bnat = const.tile([P, 3 * E], BF16, name="bnat")
+        nc.vector.memset(bnat[:], 0.0)
+        nc.scalar.dma_start(out=bnat[0:1, :], in_=b_qkv.rearrange("(o c) -> o c", o=1))
+        ctab = const.tile([P, 16, 32], BF16, name="ctab")
+        stab = const.tile([P, 16, 32], BF16, name="stab")
+        for tab_sb, tab in ((ctab, cos_tab), (stab, sin_tab)):
+            nc.scalar.dma_start(
+                out=tab_sb[:].rearrange("p (g t) j -> p g (t j)", g=4),
+                in_=tab.rearrange("(g p t) j -> p g (t j)", g=4, p=P, t=T),
+            )
+
+        x_sb = []
+        for g in range(GROUPS):
+            x_sb.append(xin.tile([P, T * E], BF16, name="x_sb%d" % g, tag="x_sb"))
+
+        def load_x(g):
+            nc.sync.dma_start(
+                out=x_sb[g][:],
+                in_=xf[512 * g : 512 * (g + 1), :].rearrange("(p t) k -> p (t k)", t=T),
+            )
+
+        wraw = const.tile([P, 4, 3 * E], BF16, name="wraw")
+
+        def load_w(c0, c1):
+            for u in range(2):
+                nc.sync.dma_start(
+                    out=wraw[:, 2 * u : 2 * u + 2, c0:c1],
+                    in_=W_qkv[256 * u : 256 * (u + 1), c0:c1].rearrange("(q e) c -> q e c", e=2),
+                )
+
+        load_x(0)
+        load_w(1024, 1536)
+        load_w(0, 1024)
+        for g in range(1, GROUPS):
+            load_x(g)
+
+        ident_f = const.tile([P, P], F32, name="ident_f")
+        make_identity(nc, ident_f[:])
+        ident_b = const.tile([P, P], BF16, name="ident_b")
+        make_identity(nc, ident_b[:])
+        ones_b = const.tile([P, P], BF16, name="ones_b")
+        nc.vector.memset(ones_b[:], 1.0)
+        perm_f = const.tile([P, P], F32, name="perm_f")
+        id4 = ident_f[:].rearrange("p (a w i) -> p a w i", a=4, w=2)
+        pm4 = perm_f[:].rearrange("p (a w i) -> p a w i", a=4, w=2)
+        nc.vector.tensor_copy(out=pm4[:, :, 0, :], in_=id4[:, :, 1, :])
+        nc.vector.tensor_copy(out=pm4[:, :, 1, :], in_=id4[:, :, 0, :])
+
+        xc = {}
+        xs = {}
+
+        def x_transposes(g):
+            xw = x_sb[g][:].bitcast(F32)
+            banks = []
+            for hf in range(2):
+                xt = pst.tile([P, 4, P], F32, name="xt", tag="t")
+                for tt in range(2):
+                    for u in range(2):
+                        c0 = 256 * (2 * hf + tt) + 128 * u
+                        nc.tensor.transpose(xt[:, 2 * tt + u, :], xw[:, c0 : c0 + 128], ident_f[:])
+                banks.append(xt)
+            return banks
+
+        def x_quantise(g, banks):
+            grouped = xgr.tile([P, 4 * 512], BF16, name="grouped", tag="grouped", align_bytes=64)
+            g32 = grouped[:].bitcast(F32)
+            for hf in range(2):
+                nc.scalar.copy(
+                    out=g32[:, 512 * hf : 512 * (hf + 1)].rearrange(
+                        "q (tt p u) -> q tt p u", tt=2, p=P, u=2
+                    ),
+                    in_=banks[hf][:].rearrange("q (tt u) p -> q tt p u", tt=2, u=2),
+                )
+            codes = xq.tile([P, 512], U32, name="xcodes", tag="xcodes", align_bytes=64)
+            scales = xq.tile([P, 512], U8, name="xscales", tag="xscales", align_bytes=64)
+            nc.vector.quantize_mx(out=codes[:].bitcast(FP8X4), scales=scales[:], in_=grouped[:])
+            xc[g] = codes
+            xs[g] = scales
+
+        banks0 = x_transposes(0)
+
+        csrep = const.tile([P, 2, 16, P], BF16, name="csrep")
+        nc.scalar.copy(
+            out=csrep[:, 0].rearrange("p a (r j) -> p a r j", r=4),
+            in_=ctab[:].unsqueeze(2).to_broadcast([P, 16, 4, 32]),
+        )
+        srep = csrep[:, 1].rearrange("p a (r w i) -> p a r w i", r=4, w=2)
+        nc.gpsimd.tensor_scalar(
+            out=srep[:, :, :, 0, :],
+            in0=stab[:, :, 16:32].unsqueeze(2).to_broadcast([P, 16, 4, 16]),
+            scalar1=1.0, scalar2=0.0, op0=ALU.mult, op1=ALU.add,
+        )
+        nc.gpsimd.tensor_scalar(
+            out=srep[:, :, :, 1, :],
+            in0=stab[:, :, 0:16].unsqueeze(2).to_broadcast([P, 16, 4, 16]),
+            scalar1=-1.0, scalar2=0.0, op0=ALU.mult, op1=ALU.add,
+        )
+
+        x_quantise(0, banks0)
+
+        wg = const.tile([P, 3 * E, 4], BF16, name="wg", align_bytes=64)
+        wc = const.tile([P, 3 * E], U32, name="wc", align_bytes=64)
+        ws = const.tile([P, 3 * E], U8, name="ws", align_bytes=64)
+
+        def w_quantise(c0):
+            nc.vector.quantize_mx(
+                out=wc[:, c0 : c0 + 512].bitcast(FP8X4),
+                scales=ws[:, c0 : c0 + 512],
+                in_=wg[:, c0 : c0 + 512, :].rearrange("q c t -> q (c t)"),
+            )
+
+        nc.vector.tensor_copy(
+            out=wg[:, VAL : VAL + 512, :].rearrange("q (c i) t -> q c t i", i=4),
+            in_=wraw[:, :, 1024:1536].rearrange("q t (c i) -> q c t i", i=4),
+        )
+        w_quantise(VAL)
+        wqk = wraw[:, :, 0:1024].rearrange("q t (g w j) -> q w g j t", g=16, w=2)
+        nc.scalar.copy(
+            out=wg[:, PAS : PAS + 512, :].rearrange("q (g j) t -> q g j t", g=16), in_=wqk[:, 1]
+        )
+        nc.vector.tensor_copy(
+            out=wg[:, ROT : ROT + 512, :].rearrange("q (g j) t -> q g j t", g=16), in_=wqk[:, 0]
+        )
+        w_quantise(PAS)
+        w_quantise(ROT)
+
+        brow = const.tile([P, 1024], BF16, name="brow")
+        bqk = bnat[:, 0:1024].rearrange("p (g w j) -> p w g j", g=16, w=2)
+        nc.vector.tensor_copy(out=brow[:, 512:1024].rearrange("p (g j) -> p g j", g=16), in_=bqk[:, 1])
+        nc.vector.tensor_copy(out=brow[:, 0:512].rearrange("p (g j) -> p g j", g=16), in_=bqk[:, 0])
+        bias_bc = const.tile([P, 1024], F32, name="bias_bc")
+        for k, rhs in enumerate((brow[:, 512:1024], bnat[:, 1024:1536])):
+            pb = psa.tile([P, 512], F32, name="pb", tag="a")
+            nc.tensor.matmul(pb[:], lhsT=ones_b[:], rhs=rhs, start=True, stop=True)
+            nc.vector.tensor_copy(out=bias_bc[:, 512 * k : 512 * (k + 1)], in_=pb[:])
+        pbt = psa.tile([P, 512], F32, name="pbt", tag="a")
+        for i in range(4):
+            nc.tensor.matmul(
+                pbt[:, 32 * i : 32 * (i + 1)], lhsT=brow[:, P * i : P * (i + 1)], rhs=ones_b[:, 0:32],
+                start=True, stop=True,
+            )
+        biasT = const.tile([P, 4], F32, name="biasT")
+        nc.vector.tensor_copy(
+            out=biasT[:], in_=pbt[:, 0:128].rearrange("p (i n) -> p i n", n=32)[:, :, 0]
+        )
+
+        csT = const.tile([P, 2, 2048], BF16, name="csT")
+        for tab in range(2):
+            for hf in range(2):
+                pt = pst.tile([P, 8, P], BF16, name="pt", tag="t")
+                for a in range(8):
+                    nc.tensor.transpose(pt[:, a, :], csrep[:, tab, 8 * hf + a, :], ident_b[:])
+                nc.scalar.copy(
+                    out=csT[:, tab, 1024 * hf : 1024 * (hf + 1)],
+                    in_=pt[:].rearrange("p a c -> p (a c)"),
+                )
+
+        oqk = {}
+        mw = {}
+
+        def mx(out, lhsT, lhsT_scale, rhs, rhs_scale):
+            nc.tensor.matmul_mx(
+                out=out, lhsT=lhsT.bitcast(FP8X4), lhsT_scale=lhsT_scale,
+                rhs=rhs.bitcast(FP8X4), rhs_scale=rhs_scale, start=True, stop=True,
+            )
+
+        def rot_block(g, i):
+            bank = psr.tile([P, 512], F32, name="rbank", tag="r")
+            cols = slice(ROT + P * i, ROT + P * (i + 1))
+            mx(bank[:], wc[:, cols], ws[:, cols], xc[g][:], xs[g][:])
+            m = mwp.tile([P, 2, 512], F32, name="mw%d" % i, tag="mw%d" % i)
+            gp = g % 4
+            nc.vector.scalar_tensor_tensor(
+                out=m[:],
+                in0=bank[:].unsqueeze(1).to_broadcast([P, 2, 512]),
+                scalar=biasT[:, i : i + 1],
+                in1=csT[:, :, 512 * gp : 512 * (gp + 1)],
+                op0=ALU.add,
+                op1=ALU.mult,
+            )
+            mw[(g, i)] = m
+
+        def token_bank(g, t, c0):
+            bank = psa.tile([P, 512], F32, name="abank", tag="a")
+            cols = slice(P * t, P * (t + 1))
+            mx(bank[:], xc[g][:, cols], xs[g][:, cols], wc[:, c0 : c0 + 512], ws[:, c0 : c0 + 512])
+            return bank
+
+        def pass_view(g, t):
+            return oqk[g][:, :, t, :].rearrange("p q (h d) -> p q h d", d=64)[:, :, :, 32:64]
+
+        def pass_view_tiles(g, t0, t1):
+            return oqk[g][:, :, t0:t1, :].rearrange("p q t (h d) -> p q t h d", d=64)[:, :, :, :, 32:64]
+
+        def group_nonrot(g):
+            ov = ovp.tile([P, T, 512], F32, name="ov", tag="ov")
+            oqk[g] = oqkp.tile([P, 2, T, 512], F32, name="oqk", tag="oqk")
+            for t in range(T):
+                bank = token_bank(g, t, VAL)
+                nc.scalar.copy(out=ov[:, t, :], in_=bank[:])
+            nc.gpsimd.tensor_tensor(
+                out=ov[:], in0=ov[:],
+                in1=bias_bc[:, 512:1024].unsqueeze(1).to_broadcast([P, T, 512]), op=ALU.add,
+            )
+            nc.sync.dma_start(
+                out=outs[2][512 * g : 512 * (g + 1), :].rearrange("(p t) c -> p (t c)", t=T),
+                in_=ov[:].rearrange("p t c -> p (t c)"),
+            )
+            bn = bias_bc[:, 0:512].rearrange("p (q h j) -> p q h j", q=2, h=8)
+            for t in range(T):
+                bank = token_bank(g, t, PAS)
+                bv = bank[:].rearrange("p (q h j) -> p q h j", q=2, h=8)
+                if t in N_ON_VECTOR:
+                    nc.vector.tensor_tensor(out=pass_view(g, t), in0=bv, in1=bn, op=ALU.add)
+                else:
+                    nc.scalar.copy(out=pass_view(g, t), in_=bv)
+            nc.gpsimd.tensor_tensor(
+                out=pass_view_tiles(g, 0, 2), in0=pass_view_tiles(g, 0, 2),
+                in1=bias_bc[:, 0:512].rearrange("p (q o h j) -> p q o h j", q=2, o=1, h=8).to_broadcast([P, 2, 2, 8, 32]),
+                op=ALU.add,
+            )
+
+        def group_rot(g):
+            for i in range(4):
+                rot_block(g, i)
+
+        def group_back(g):
+            for t in range(T):
+                bt = pst.tile([P, 512], F32, name="bt", tag="t")
+                for i in range(4):
+                    dst = bt[:, P * i : P * (i + 1)]
+                    nc.tensor.matmul(
+                        dst, lhsT=mw[(g, i)][:, 0, P * t : P * (t + 1)], rhs=ident_f[:],
+                        is_transpose=True, start=True, stop=False,
+                    )
+                    nc.tensor.matmul(
+                        dst, lhsT=mw[(g, i)][:, 1, P * t : P * (t + 1)], rhs=perm_f[:],
+                        is_transpose=True, start=False, stop=True,
+                    )
+                nc.scalar.copy(
+                    out=oqk[g][:, :, t, :].rearrange("p q (h d) -> p q h d", d=64)[:, :, :, 0:32],
+                    in_=bt[:].rearrange("p (q h j) -> p q h j", q=2, h=8),
+                )
+            for q in range(2):
+                nc.sync.dma_start(
+                    out=outs[q][512 * g : 512 * (g + 1), :].rearrange("(p t) c -> p (t c)", t=T),
+                    in_=oqk[g][:, q].rearrange("p t c -> p (t c)"),
+                )
+
+        for g in range(GROUPS):
+            if g == 0:
+                group_nonrot(g)
+                group_rot(g)
+            else:
+                group_rot(g)
+                group_nonrot(g)
+            if g + 1 < GROUPS:
+                x_quantise(g + 1, x_transposes(g + 1))
+            if g >= 1:
+                group_back(g - 1)
+        group_back(GROUPS - 1)

@@ -41,16 +41,18 @@ def tile_improvedattention_pa_t_kernel(
         pst = ctx.enter_context(tc.psum_pool(name="pst", bufs=3))
         ctx.enter_context(nc.allow_non_contiguous_dma(reason="short rows of tables and column chunks"))
 
+        ctx.enter_context(tc.manual_schedule())
+
         bnat = const.tile([P, 3 * E], BF16, name="bnat")
         nc.vector.memset(bnat[:], 0.0)
-        nc.scalar.dma_start(out=bnat[0:1, :], in_=b_qkv.rearrange("(o c) -> o c", o=1))
         ctab = const.tile([P, 16, 32], BF16, name="ctab")
         stab = const.tile([P, 16, 32], BF16, name="stab")
-        for tab_sb, tab in ((ctab, cos_tab), (stab, sin_tab)):
+        for tab_sb, tab in ((stab, sin_tab), (ctab, cos_tab)):
             nc.scalar.dma_start(
                 out=tab_sb[:].rearrange("p (g t) j -> p g (t j)", g=4),
                 in_=tab.rearrange("(g p t) j -> p g (t j)", g=4, p=P, t=T),
             )
+        nc.scalar.dma_start(out=bnat[0:1, :], in_=b_qkv.rearrange("(o c) -> o c", o=1))
 
         x_sb = []
         for g in range(GROUPS):
@@ -91,6 +93,8 @@ def tile_improvedattention_pa_t_kernel(
 
         xc = {}
         xs = {}
+        xbanks = {}
+        xgrouped = {}
 
         def x_transposes(g):
             xw = x_sb[g][:].bitcast(F32)
@@ -102,9 +106,9 @@ def tile_improvedattention_pa_t_kernel(
                         c0 = 256 * (2 * hf + tt) + 128 * u
                         nc.tensor.transpose(xt[:, 2 * tt + u, :], xw[:, c0 : c0 + 128], ident_f[:])
                 banks.append(xt)
-            return banks
+            xbanks[g] = banks
 
-        def x_quantise(g, banks):
+        def x_copy_out(g):
             grouped = xgr.tile([P, 4 * 512], BF16, name="grouped", tag="grouped", align_bytes=64)
             g32 = grouped[:].bitcast(F32)
             for hf in range(2):
@@ -112,34 +116,50 @@ def tile_improvedattention_pa_t_kernel(
                     out=g32[:, 512 * hf : 512 * (hf + 1)].rearrange(
                         "q (tt p u) -> q tt p u", tt=2, p=P, u=2
                     ),
-                    in_=banks[hf][:].rearrange("q (tt u) p -> q tt p u", tt=2, u=2),
+                    in_=xbanks[g][hf][:].rearrange("q (tt u) p -> q tt p u", tt=2, u=2),
                 )
+            xgrouped[g] = grouped
+
+        def x_quantise(g):
             codes = xq.tile([P, 512], U32, name="xcodes", tag="xcodes", align_bytes=64)
             scales = xq.tile([P, 512], U8, name="xscales", tag="xscales", align_bytes=64)
-            nc.vector.quantize_mx(out=codes[:].bitcast(FP8X4), scales=scales[:], in_=grouped[:])
+            nc.vector.quantize_mx(out=codes[:].bitcast(FP8X4), scales=scales[:], in_=xgrouped[g][:])
             xc[g] = codes
             xs[g] = scales
 
-        banks0 = x_transposes(0)
+        x_transposes(0)
 
         csrep = const.tile([P, 2, 16, P], BF16, name="csrep")
+        srep = csrep[:, 1].rearrange("p a (r w i) -> p a r w i", r=4, w=2)
+        nc.vector.tensor_copy(
+            out=srep[:, :, :, 0, :], in_=stab[:, :, 16:32].unsqueeze(2).to_broadcast([P, 16, 4, 16])
+        )
+        nc.vector.tensor_scalar_mul(
+            out=srep[:, :, :, 1, :],
+            in0=stab[:, :, 0:16].unsqueeze(2).to_broadcast([P, 16, 4, 16]),
+            scalar1=-1.0,
+        )
         nc.scalar.copy(
             out=csrep[:, 0].rearrange("p a (r j) -> p a r j", r=4),
             in_=ctab[:].unsqueeze(2).to_broadcast([P, 16, 4, 32]),
         )
-        srep = csrep[:, 1].rearrange("p a (r w i) -> p a r w i", r=4, w=2)
-        nc.gpsimd.tensor_scalar(
-            out=srep[:, :, :, 0, :],
-            in0=stab[:, :, 16:32].unsqueeze(2).to_broadcast([P, 16, 4, 16]),
-            scalar1=1.0, scalar2=0.0, op0=ALU.mult, op1=ALU.add,
-        )
-        nc.gpsimd.tensor_scalar(
-            out=srep[:, :, :, 1, :],
-            in0=stab[:, :, 0:16].unsqueeze(2).to_broadcast([P, 16, 4, 16]),
-            scalar1=-1.0, scalar2=0.0, op0=ALU.mult, op1=ALU.add,
-        )
+        x_copy_out(0)
 
-        x_quantise(0, banks0)
+        brow = const.tile([P, 1024], BF16, name="brow")
+        bqk = bnat[:, 0:1024].rearrange("p (g w j) -> p w g j", g=16, w=2)
+        nc.vector.tensor_copy(out=brow[:, 512:1024].rearrange("p (g j) -> p g j", g=16), in_=bqk[:, 1])
+        nc.vector.tensor_copy(out=brow[:, 0:512].rearrange("p (g j) -> p g j", g=16), in_=bqk[:, 0])
+        pbs = []
+        for rhs in (brow[:, 512:1024], bnat[:, 1024:1536]):
+            pb = psa.tile([P, 512], F32, name="pb", tag="a")
+            nc.tensor.matmul(pb[:], lhsT=ones_b[:], rhs=rhs, start=True, stop=True)
+            pbs.append(pb)
+        pbt = psa.tile([P, 512], F32, name="pbt", tag="a")
+        for i in range(4):
+            nc.tensor.matmul(
+                pbt[:, 32 * i : 32 * (i + 1)], lhsT=brow[:, P * i : P * (i + 1)], rhs=ones_b[:, 0:32],
+                start=True, stop=True,
+            )
 
         wg = const.tile([P, 3 * E, 4], BF16, name="wg", align_bytes=64)
         wc = const.tile([P, 3 * E], U32, name="wc", align_bytes=64)
@@ -156,49 +176,46 @@ def tile_improvedattention_pa_t_kernel(
             out=wg[:, VAL : VAL + 512, :].rearrange("q (c i) t -> q c t i", i=4),
             in_=wraw[:, :, 1024:1536].rearrange("q t (c i) -> q c t i", i=4),
         )
-        w_quantise(VAL)
-        wqk = wraw[:, :, 0:1024].rearrange("q t (g w j) -> q w g j t", g=16, w=2)
-        nc.scalar.copy(
-            out=wg[:, PAS : PAS + 512, :].rearrange("q (g j) t -> q g j t", g=16), in_=wqk[:, 1]
-        )
-        nc.vector.tensor_copy(
-            out=wg[:, ROT : ROT + 512, :].rearrange("q (g j) t -> q g j t", g=16), in_=wqk[:, 0]
-        )
-        w_quantise(PAS)
-        w_quantise(ROT)
-
-        brow = const.tile([P, 1024], BF16, name="brow")
-        bqk = bnat[:, 0:1024].rearrange("p (g w j) -> p w g j", g=16, w=2)
-        nc.vector.tensor_copy(out=brow[:, 512:1024].rearrange("p (g j) -> p g j", g=16), in_=bqk[:, 1])
-        nc.vector.tensor_copy(out=brow[:, 0:512].rearrange("p (g j) -> p g j", g=16), in_=bqk[:, 0])
-        bias_bc = const.tile([P, 1024], F32, name="bias_bc")
-        for k, rhs in enumerate((brow[:, 512:1024], bnat[:, 1024:1536])):
-            pb = psa.tile([P, 512], F32, name="pb", tag="a")
-            nc.tensor.matmul(pb[:], lhsT=ones_b[:], rhs=rhs, start=True, stop=True)
-            nc.vector.tensor_copy(out=bias_bc[:, 512 * k : 512 * (k + 1)], in_=pb[:])
-        pbt = psa.tile([P, 512], F32, name="pbt", tag="a")
-        for i in range(4):
-            nc.tensor.matmul(
-                pbt[:, 32 * i : 32 * (i + 1)], lhsT=brow[:, P * i : P * (i + 1)], rhs=ones_b[:, 0:32],
-                start=True, stop=True,
-            )
         biasT = const.tile([P, 4], F32, name="biasT")
         nc.vector.tensor_copy(
             out=biasT[:], in_=pbt[:, 0:128].rearrange("p (i n) -> p i n", n=32)[:, :, 0]
         )
+        w_quantise(VAL)
+        x_quantise(0)
 
         csT = const.tile([P, 2, 2048], BF16, name="csT")
-        for tab in range(2):
-            for hf in range(2):
-                pt = pst.tile([P, 8, P], BF16, name="pt", tag="t")
-                for a in range(8):
-                    nc.tensor.transpose(pt[:, a, :], csrep[:, tab, 8 * hf + a, :], ident_b[:])
-                nc.scalar.copy(
-                    out=csT[:, tab, 1024 * hf : 1024 * (hf + 1)],
-                    in_=pt[:].rearrange("p a c -> p (a c)"),
-                )
+
+        def table_bank(tab, hf):
+            pt = pst.tile([P, 8, P], BF16, name="pt", tag="t")
+            for a in range(8):
+                nc.tensor.transpose(pt[:, a, :], csrep[:, tab, 8 * hf + a, :], ident_b[:])
+            nc.scalar.copy(
+                out=csT[:, tab, 1024 * hf : 1024 * (hf + 1)], in_=pt[:].rearrange("p a c -> p (a c)")
+            )
+
+        table_bank(1, 0)
+        table_bank(1, 1)
+        wqk = wraw[:, :, 0:1024].rearrange("q t (g w j) -> q w g j t", g=16, w=2)
+        nc.vector.tensor_copy(
+            out=wg[:, ROT : ROT + 512, :].rearrange("q (g j) t -> q g j t", g=16), in_=wqk[:, 0]
+        )
+        nc.scalar.copy(
+            out=wg[:, PAS + 256 : PAS + 512, :].rearrange("q (g j) t -> q g j t", g=8),
+            in_=wqk[:, 1, 8:16],
+        )
+        nc.vector.tensor_copy(
+            out=wg[:, PAS : PAS + 256, :].rearrange("q (g j) t -> q g j t", g=8), in_=wqk[:, 1, 0:8]
+        )
+        w_quantise(ROT)
+        w_quantise(PAS)
+        table_bank(0, 0)
+        table_bank(0, 1)
+        bias_bc = const.tile([P, 1024], F32, name="bias_bc")
+        for k in range(2):
+            nc.scalar.copy(out=bias_bc[:, 512 * k : 512 * (k + 1)], in_=pbs[k][:])
 
         oqk = {}
+        ovs = {}
         mw = {}
 
         def mx(out, lhsT, lhsT_scale, rhs, rhs_scale):
@@ -235,70 +252,101 @@ def tile_improvedattention_pa_t_kernel(
         def pass_view_tiles(g, t0, t1):
             return oqk[g][:, :, t0:t1, :].rearrange("p q t (h d) -> p q t h d", d=64)[:, :, :, :, 32:64]
 
-        def group_nonrot(g):
-            ov = ovp.tile([P, T, 512], F32, name="ov", tag="ov")
-            oqk[g] = oqkp.tile([P, 2, T, 512], F32, name="oqk", tag="oqk")
-            for t in range(T):
-                bank = token_bank(g, t, VAL)
-                nc.scalar.copy(out=ov[:, t, :], in_=bank[:])
+        def out_rows(q, g):
+            return outs[q][512 * g : 512 * (g + 1), :]
+
+        def value_tile(g, t):
+            if t == 0:
+                ovs[g] = ovp.tile([P, T, 512], F32, name="ov", tag="ov")
+            bank = token_bank(g, t, VAL)
+            nc.scalar.copy(out=ovs[g][:, t, :], in_=bank[:])
+
+        def value_finish(g):
+            ov = ovs[g]
             nc.gpsimd.tensor_tensor(
                 out=ov[:], in0=ov[:],
                 in1=bias_bc[:, 512:1024].unsqueeze(1).to_broadcast([P, T, 512]), op=ALU.add,
             )
             nc.sync.dma_start(
-                out=outs[2][512 * g : 512 * (g + 1), :].rearrange("(p t) c -> p (t c)", t=T),
+                out=out_rows(2, g).rearrange("(p t) c -> p (t c)", t=T),
                 in_=ov[:].rearrange("p t c -> p (t c)"),
             )
-            bn = bias_bc[:, 0:512].rearrange("p (q h j) -> p q h j", q=2, h=8)
-            for t in range(T):
-                bank = token_bank(g, t, PAS)
-                bv = bank[:].rearrange("p (q h j) -> p q h j", q=2, h=8)
-                if t in N_ON_VECTOR:
-                    nc.vector.tensor_tensor(out=pass_view(g, t), in0=bv, in1=bn, op=ALU.add)
-                else:
-                    nc.scalar.copy(out=pass_view(g, t), in_=bv)
+
+        def pass_tile(g, t):
+            if t == 0:
+                oqk[g] = oqkp.tile([P, 2, T, 512], F32, name="oqk", tag="oqk")
+            bank = token_bank(g, t, PAS)
+            bv = bank[:].rearrange("p (q h j) -> p q h j", q=2, h=8)
+            if t in N_ON_VECTOR:
+                bn = bias_bc[:, 0:512].rearrange("p (q h j) -> p q h j", q=2, h=8)
+                nc.vector.tensor_tensor(out=pass_view(g, t), in0=bv, in1=bn, op=ALU.add)
+            else:
+                nc.scalar.copy(out=pass_view(g, t), in_=bv)
+
+        def pass_finish(g):
             nc.gpsimd.tensor_tensor(
                 out=pass_view_tiles(g, 0, 2), in0=pass_view_tiles(g, 0, 2),
                 in1=bias_bc[:, 0:512].rearrange("p (q o h j) -> p q o h j", q=2, o=1, h=8).to_broadcast([P, 2, 2, 8, 32]),
                 op=ALU.add,
             )
 
-        def group_rot(g):
+        def back_tile(g, t, store_now):
+            bt = pst.tile([P, 512], F32, name="bt", tag="t")
             for i in range(4):
-                rot_block(g, i)
-
-        def group_back(g):
-            for t in range(T):
-                bt = pst.tile([P, 512], F32, name="bt", tag="t")
-                for i in range(4):
-                    dst = bt[:, P * i : P * (i + 1)]
-                    nc.tensor.matmul(
-                        dst, lhsT=mw[(g, i)][:, 0, P * t : P * (t + 1)], rhs=ident_f[:],
-                        is_transpose=True, start=True, stop=False,
-                    )
-                    nc.tensor.matmul(
-                        dst, lhsT=mw[(g, i)][:, 1, P * t : P * (t + 1)], rhs=perm_f[:],
-                        is_transpose=True, start=False, stop=True,
-                    )
-                nc.scalar.copy(
-                    out=oqk[g][:, :, t, :].rearrange("p q (h d) -> p q h d", d=64)[:, :, :, 0:32],
-                    in_=bt[:].rearrange("p (q h j) -> p q h j", q=2, h=8),
+                dst = bt[:, P * i : P * (i + 1)]
+                nc.tensor.matmul(
+                    dst, lhsT=mw[(g, i)][:, 0, P * t : P * (t + 1)], rhs=ident_f[:],
+                    is_transpose=True, start=True, stop=False,
                 )
+                nc.tensor.matmul(
+                    dst, lhsT=mw[(g, i)][:, 1, P * t : P * (t + 1)], rhs=perm_f[:],
+                    is_transpose=True, start=False, stop=True,
+                )
+            nc.scalar.copy(
+                out=oqk[g][:, :, t, :].rearrange("p q (h d) -> p q h d", d=64)[:, :, :, 0:32],
+                in_=bt[:].rearrange("p (q h j) -> p q h j", q=2, h=8),
+            )
+            if store_now:
+                for q in range(2):
+                    nc.sync.dma_start(
+                        out=out_rows(q, g).rearrange("(p t) c -> p t c", t=T)[:, t, :],
+                        in_=oqk[g][:, q, t, :],
+                    )
+
+        def store_qk(g):
             for q in range(2):
                 nc.sync.dma_start(
-                    out=outs[q][512 * g : 512 * (g + 1), :].rearrange("(p t) c -> p (t c)", t=T),
+                    out=out_rows(q, g).rearrange("(p t) c -> p (t c)", t=T),
                     in_=oqk[g][:, q].rearrange("p t c -> p (t c)"),
                 )
 
+        FIRST = ("v0", "v1", "v2", "v3", "gv", "n0", "n1", "gn", "r0", "n2", "r1", "n3", "r2", "r3", "X", "xe", "Q")
+        STEADY = ("r0", "v0", "v1", "r1", "v2", "v3", "gv", "r2", "n0", "n1", "gn", "r3", "n2", "n3", "X", "xe", "Q", "B0", "B1", "B2", "B3", "sq")
         for g in range(GROUPS):
-            if g == 0:
-                group_nonrot(g)
-                group_rot(g)
-            else:
-                group_rot(g)
-                group_nonrot(g)
-            if g + 1 < GROUPS:
-                x_quantise(g + 1, x_transposes(g + 1))
-            if g >= 1:
-                group_back(g - 1)
-        group_back(GROUPS - 1)
+            for tok in FIRST if g == 0 else STEADY:
+                k = tok[0]
+                if tok == "gv":
+                    value_finish(g)
+                elif tok == "gn":
+                    pass_finish(g)
+                elif tok == "sq":
+                    store_qk(g - 1)
+                elif tok == "xe":
+                    if g + 1 < GROUPS:
+                        x_copy_out(g + 1)
+                elif k == "X":
+                    if g + 1 < GROUPS:
+                        x_transposes(g + 1)
+                elif k == "Q":
+                    if g + 1 < GROUPS:
+                        x_quantise(g + 1)
+                elif k == "r":
+                    rot_block(g, int(tok[1]))
+                elif k == "v":
+                    value_tile(g, int(tok[1]))
+                elif k == "n":
+                    pass_tile(g, int(tok[1]))
+                elif k == "B":
+                    back_tile(g - 1, int(tok[1]), False)
+        for t in range(T):
+            back_tile(GROUPS - 1, t, True)

@@ -320,8 +320,8 @@ def tile_improvedattention_pa_t_kernel(
                     in_=oqk[g][:, q].rearrange("p t c -> p (t c)"),
                 )
 
-        FIRST = ("v0", "v1", "v2", "v3", "gv", "n0", "n1", "gn", "r0", "n2", "r1", "n3", "r2", "r3", "X", "xe", "Q")
-        STEADY = ("r0", "v0", "v1", "r1", "v2", "v3", "gv", "r2", "n0", "n1", "gn", "r3", "n2", "n3", "X", "xe", "Q", "B0", "B1", "B2", "B3", "sq")
+        FIRST = ("v0", "v1", "v2", "v3", "gv", "X", "xe", "n0", "n1", "gn", "Q", "r0", "n2", "r1", "n3", "r2", "r3")
+        STEADY = ("r0", "r1", "v0", "v1", "X", "xe", "B0", "r2", "v2", "v3", "gv", "n0", "Q", "B1", "B2", "r3", "n1", "gn", "n2", "n3", "B3", "sq")
         for g in range(GROUPS):
             for tok in FIRST if g == 0 else STEADY:
                 k = tok[0]

@@ -18,7 +18,6 @@ T = 4
 FLOPS = 2 * TOKENS * E * 3 * E
 
 ROT, PAS, VAL = 0, 512, 1024
-N_ON_VECTOR = (2, 3)
 
 
 def tile_improvedattention_pa_t_kernel(
@@ -40,19 +39,18 @@ def tile_improvedattention_pa_t_kernel(
         psa = ctx.enter_context(tc.psum_pool(name="psa", bufs=3))
         pst = ctx.enter_context(tc.psum_pool(name="pst", bufs=3))
         ctx.enter_context(nc.allow_non_contiguous_dma(reason="short rows of tables and column chunks"))
-
         ctx.enter_context(tc.manual_schedule())
 
         bnat = const.tile([P, 3 * E], BF16, name="bnat")
         nc.vector.memset(bnat[:], 0.0)
         ctab = const.tile([P, 16, 32], BF16, name="ctab")
         stab = const.tile([P, 16, 32], BF16, name="stab")
+        nc.scalar.dma_start(out=bnat[0:1, :], in_=b_qkv.rearrange("(o c) -> o c", o=1))
         for tab_sb, tab in ((stab, sin_tab), (ctab, cos_tab)):
             nc.scalar.dma_start(
                 out=tab_sb[:].rearrange("p (g t) j -> p g (t j)", g=4),
                 in_=tab.rearrange("(g p t) j -> p g (t j)", g=4, p=P, t=T),
             )
-        nc.scalar.dma_start(out=bnat[0:1, :], in_=b_qkv.rearrange("(o c) -> o c", o=1))
 
         x_sb = []
         for g in range(GROUPS):
@@ -66,16 +64,17 @@ def tile_improvedattention_pa_t_kernel(
 
         wraw = const.tile([P, 4, 3 * E], BF16, name="wraw")
 
-        def load_w(c0, c1):
+        def load_w(c0):
             for u in range(2):
                 nc.sync.dma_start(
-                    out=wraw[:, 2 * u : 2 * u + 2, c0:c1],
-                    in_=W_qkv[256 * u : 256 * (u + 1), c0:c1].rearrange("(q e) c -> q e c", e=2),
+                    out=wraw[:, 2 * u : 2 * u + 2, c0 : c0 + 512],
+                    in_=W_qkv[256 * u : 256 * (u + 1), c0 : c0 + 512].rearrange("(q e) c -> q e c", e=2),
                 )
 
         load_x(0)
-        load_w(1024, 1536)
-        load_w(0, 1024)
+        load_w(1024)
+        load_w(0)
+        load_w(512)
         for g in range(1, GROUPS):
             load_x(g)
 
@@ -127,24 +126,6 @@ def tile_improvedattention_pa_t_kernel(
             xc[g] = codes
             xs[g] = scales
 
-        x_transposes(0)
-
-        csrep = const.tile([P, 2, 16, P], BF16, name="csrep")
-        srep = csrep[:, 1].rearrange("p a (r w i) -> p a r w i", r=4, w=2)
-        nc.vector.tensor_copy(
-            out=srep[:, :, :, 0, :], in_=stab[:, :, 16:32].unsqueeze(2).to_broadcast([P, 16, 4, 16])
-        )
-        nc.vector.tensor_scalar_mul(
-            out=srep[:, :, :, 1, :],
-            in0=stab[:, :, 0:16].unsqueeze(2).to_broadcast([P, 16, 4, 16]),
-            scalar1=-1.0,
-        )
-        nc.scalar.copy(
-            out=csrep[:, 0].rearrange("p a (r j) -> p a r j", r=4),
-            in_=ctab[:].unsqueeze(2).to_broadcast([P, 16, 4, 32]),
-        )
-        x_copy_out(0)
-
         brow = const.tile([P, 1024], BF16, name="brow")
         bqk = bnat[:, 0:1024].rearrange("p (g w j) -> p w g j", g=16, w=2)
         nc.vector.tensor_copy(out=brow[:, 512:1024].rearrange("p (g j) -> p g j", g=16), in_=bqk[:, 1])
@@ -160,6 +141,48 @@ def tile_improvedattention_pa_t_kernel(
                 pbt[:, 32 * i : 32 * (i + 1)], lhsT=brow[:, P * i : P * (i + 1)], rhs=ones_b[:, 0:32],
                 start=True, stop=True,
             )
+
+        csrep = const.tile([P, 2, 16, P], BF16, name="csrep")
+        csT = const.tile([P, 2, 2048], BF16, name="csT")
+        crep = csrep[:, 0].rearrange("p a (r j) -> p a r j", r=4)
+        srep = csrep[:, 1].rearrange("p a (r w i) -> p a r w i", r=4, w=2)
+
+        def spread(tab_part, n, width):
+            return tab_part.unsqueeze(2).to_broadcast([P, n, 4, width])
+
+        nc.vector.tensor_copy(out=srep[:, 0:4, :, 0, :], in_=spread(stab[:, 0:4, 16:32], 4, 16))
+        nc.vector.tensor_scalar_mul(
+            out=srep[:, 0:4, :, 1, :], in0=spread(stab[:, 0:4, 0:16], 4, 16), scalar1=-1.0
+        )
+        nc.scalar.copy(out=crep[:, 0:4], in_=spread(ctab[:, 0:4, :], 4, 32))
+        nc.gpsimd.tensor_scalar(
+            out=crep[:, 4:16], in0=spread(ctab[:, 4:16, :], 12, 32),
+            scalar1=1.0, scalar2=0.0, op0=ALU.mult, op1=ALU.add,
+        )
+        nc.gpsimd.tensor_scalar(
+            out=srep[:, 4:16, :, 0, :], in0=spread(stab[:, 4:16, 16:32], 12, 16),
+            scalar1=1.0, scalar2=0.0, op0=ALU.mult, op1=ALU.add,
+        )
+        nc.gpsimd.tensor_scalar(
+            out=srep[:, 4:16, :, 1, :], in0=spread(stab[:, 4:16, 0:16], 12, 16),
+            scalar1=-1.0, scalar2=0.0, op0=ALU.mult, op1=ALU.add,
+        )
+
+        def table_part(gp):
+            pt = pst.tile([P, 2, T, P], BF16, name="pt", tag="t")
+            for tab in range(2):
+                for t in range(T):
+                    nc.tensor.transpose(pt[:, tab, t, :], csrep[:, tab, T * gp + t, :], ident_b[:])
+            nc.scalar.copy(
+                out=csT[:, :, 512 * gp : 512 * (gp + 1)], in_=pt[:].rearrange("p b t c -> p b (t c)")
+            )
+
+        bias_bc = const.tile([P, 1024], F32, name="bias_bc")
+        for k in range(2):
+            nc.scalar.copy(out=bias_bc[:, 512 * k : 512 * (k + 1)], in_=pbs[k][:])
+        x_transposes(0)
+        x_copy_out(0)
+        table_part(0)
 
         wg = const.tile([P, 3 * E, 4], BF16, name="wg", align_bytes=64)
         wc = const.tile([P, 3 * E], U32, name="wc", align_bytes=64)
@@ -182,41 +205,24 @@ def tile_improvedattention_pa_t_kernel(
         )
         w_quantise(VAL)
         x_quantise(0)
-
-        csT = const.tile([P, 2, 2048], BF16, name="csT")
-
-        def table_bank(tab, hf):
-            pt = pst.tile([P, 8, P], BF16, name="pt", tag="t")
-            for a in range(8):
-                nc.tensor.transpose(pt[:, a, :], csrep[:, tab, 8 * hf + a, :], ident_b[:])
-            nc.scalar.copy(
-                out=csT[:, tab, 1024 * hf : 1024 * (hf + 1)], in_=pt[:].rearrange("p a c -> p (a c)")
-            )
-
-        table_bank(1, 0)
-        table_bank(1, 1)
         wqk = wraw[:, :, 0:1024].rearrange("q t (g w j) -> q w g j t", g=16, w=2)
-        nc.vector.tensor_copy(
-            out=wg[:, ROT : ROT + 512, :].rearrange("q (g j) t -> q g j t", g=16), in_=wqk[:, 0]
-        )
-        nc.scalar.copy(
-            out=wg[:, PAS + 256 : PAS + 512, :].rearrange("q (g j) t -> q g j t", g=8),
-            in_=wqk[:, 1, 8:16],
-        )
-        nc.vector.tensor_copy(
-            out=wg[:, PAS : PAS + 256, :].rearrange("q (g j) t -> q g j t", g=8), in_=wqk[:, 1, 0:8]
-        )
+        for hf in range(2):
+            gs = slice(8 * hf, 8 * (hf + 1))
+            nc.vector.tensor_copy(
+                out=wg[:, ROT + 256 * hf : ROT + 256 * (hf + 1), :].rearrange("q (g j) t -> q g j t", g=8),
+                in_=wqk[:, 0, gs],
+            )
+            nc.scalar.copy(
+                out=wg[:, PAS + 256 * hf : PAS + 256 * (hf + 1), :].rearrange("q (g j) t -> q g j t", g=8),
+                in_=wqk[:, 1, gs],
+            )
         w_quantise(ROT)
         w_quantise(PAS)
-        table_bank(0, 0)
-        table_bank(0, 1)
-        bias_bc = const.tile([P, 1024], F32, name="bias_bc")
-        for k in range(2):
-            nc.scalar.copy(out=bias_bc[:, 512 * k : 512 * (k + 1)], in_=pbs[k][:])
 
         oqk = {}
         ovs = {}
         mw = {}
+        bts = {}
 
         def mx(out, lhsT, lhsT_scale, rhs, rhs_scale):
             nc.tensor.matmul_mx(
@@ -246,14 +252,8 @@ def tile_improvedattention_pa_t_kernel(
             mx(bank[:], xc[g][:, cols], xs[g][:, cols], wc[:, c0 : c0 + 512], ws[:, c0 : c0 + 512])
             return bank
 
-        def pass_view(g, t):
-            return oqk[g][:, :, t, :].rearrange("p q (h d) -> p q h d", d=64)[:, :, :, 32:64]
-
-        def pass_view_tiles(g, t0, t1):
-            return oqk[g][:, :, t0:t1, :].rearrange("p q t (h d) -> p q t h d", d=64)[:, :, :, :, 32:64]
-
-        def out_rows(q, g):
-            return outs[q][512 * g : 512 * (g + 1), :]
+        def out_rows(q, g, t0):
+            return outs[q][512 * g : 512 * (g + 1), :].rearrange("(p t) c -> p t c", t=T)[:, t0 : t0 + 2, :]
 
         def value_tile(g, t):
             if t == 0:
@@ -261,92 +261,96 @@ def tile_improvedattention_pa_t_kernel(
             bank = token_bank(g, t, VAL)
             nc.scalar.copy(out=ovs[g][:, t, :], in_=bank[:])
 
-        def value_finish(g):
-            ov = ovs[g]
+        def value_finish(g, t0):
+            ov = ovs[g][:, t0 : t0 + 2, :]
             nc.gpsimd.tensor_tensor(
-                out=ov[:], in0=ov[:],
-                in1=bias_bc[:, 512:1024].unsqueeze(1).to_broadcast([P, T, 512]), op=ALU.add,
+                out=ov, in0=ov, in1=bias_bc[:, 512:1024].unsqueeze(1).to_broadcast([P, 2, 512]), op=ALU.add
             )
-            nc.sync.dma_start(
-                out=out_rows(2, g).rearrange("(p t) c -> p (t c)", t=T),
-                in_=ov[:].rearrange("p t c -> p (t c)"),
-            )
+            nc.sync.dma_start(out=out_rows(2, g, t0), in_=ov)
 
         def pass_tile(g, t):
             if t == 0:
                 oqk[g] = oqkp.tile([P, 2, T, 512], F32, name="oqk", tag="oqk")
             bank = token_bank(g, t, PAS)
             bv = bank[:].rearrange("p (q h j) -> p q h j", q=2, h=8)
-            if t in N_ON_VECTOR:
+            dst = oqk[g][:, :, t, :].rearrange("p q (h d) -> p q h d", d=64)[:, :, :, 32:64]
+            if t >= 2:
                 bn = bias_bc[:, 0:512].rearrange("p (q h j) -> p q h j", q=2, h=8)
-                nc.vector.tensor_tensor(out=pass_view(g, t), in0=bv, in1=bn, op=ALU.add)
+                nc.vector.tensor_tensor(out=dst, in0=bv, in1=bn, op=ALU.add)
             else:
-                nc.scalar.copy(out=pass_view(g, t), in_=bv)
+                nc.scalar.copy(out=dst, in_=bv)
 
         def pass_finish(g):
+            dst = oqk[g][:, :, 0:2, :].rearrange("p q t (h d) -> p q t h d", d=64)[:, :, :, :, 32:64]
             nc.gpsimd.tensor_tensor(
-                out=pass_view_tiles(g, 0, 2), in0=pass_view_tiles(g, 0, 2),
+                out=dst, in0=dst,
                 in1=bias_bc[:, 0:512].rearrange("p (q o h j) -> p q o h j", q=2, o=1, h=8).to_broadcast([P, 2, 2, 8, 32]),
                 op=ALU.add,
             )
 
-        def back_tile(g, t, store_now):
-            bt = pst.tile([P, 512], F32, name="bt", tag="t")
-            for i in range(4):
-                dst = bt[:, P * i : P * (i + 1)]
-                nc.tensor.matmul(
-                    dst, lhsT=mw[(g, i)][:, 0, P * t : P * (t + 1)], rhs=ident_f[:],
-                    is_transpose=True, start=True, stop=False,
-                )
-                nc.tensor.matmul(
-                    dst, lhsT=mw[(g, i)][:, 1, P * t : P * (t + 1)], rhs=perm_f[:],
-                    is_transpose=True, start=False, stop=True,
-                )
-            nc.scalar.copy(
-                out=oqk[g][:, :, t, :].rearrange("p q (h d) -> p q h d", d=64)[:, :, :, 0:32],
-                in_=bt[:].rearrange("p (q h j) -> p q h j", q=2, h=8),
-            )
-            if store_now:
-                for q in range(2):
-                    nc.sync.dma_start(
-                        out=out_rows(q, g).rearrange("(p t) c -> p t c", t=T)[:, t, :],
-                        in_=oqk[g][:, q, t, :],
-                    )
+        def back_half(g, t0, i0):
+            if i0 == 0:
+                for t in (t0, t0 + 1):
+                    bts[t] = pst.tile([P, 512], F32, name="bt", tag="t")
+            for i in (i0, i0 + 1):
+                for part, moving in ((0, ident_f), (1, perm_f)):
+                    for t in (t0, t0 + 1):
+                        nc.tensor.matmul(
+                            bts[t][:, P * i : P * (i + 1)],
+                            lhsT=mw[(g, i)][:, part, P * t : P * (t + 1)], rhs=moving[:],
+                            is_transpose=True, start=(part == 0), stop=(part == 1),
+                        )
 
-        def store_qk(g):
+        def back_finish(g, t0):
+            for t in (t0, t0 + 1):
+                nc.scalar.copy(
+                    out=oqk[g][:, :, t, :].rearrange("p q (h d) -> p q h d", d=64)[:, :, :, 0:32],
+                    in_=bts[t][:].rearrange("p (q h j) -> p q h j", q=2, h=8),
+                )
             for q in range(2):
-                nc.sync.dma_start(
-                    out=out_rows(q, g).rearrange("(p t) c -> p (t c)", t=T),
-                    in_=oqk[g][:, q].rearrange("p t c -> p (t c)"),
-                )
+                nc.sync.dma_start(out=out_rows(q, g, t0), in_=oqk[g][:, q, t0 : t0 + 2, :])
 
-        FIRST = ("v0", "v1", "v2", "v3", "gv", "X", "xe", "n0", "n1", "gn", "Q", "r0", "n2", "r1", "n3", "r2", "r3")
-        STEADY = ("r0", "r1", "v0", "v1", "X", "xe", "B0", "r2", "v2", "v3", "gv", "n0", "Q", "B1", "B2", "r3", "n1", "gn", "n2", "n3", "B3", "sq")
-        for g in range(GROUPS):
-            for tok in FIRST if g == 0 else STEADY:
-                k = tok[0]
-                if tok == "gv":
-                    value_finish(g)
-                elif tok == "gn":
-                    pass_finish(g)
-                elif tok == "sq":
-                    store_qk(g - 1)
-                elif tok == "xe":
-                    if g + 1 < GROUPS:
-                        x_copy_out(g + 1)
-                elif k == "X":
-                    if g + 1 < GROUPS:
-                        x_transposes(g + 1)
-                elif k == "Q":
-                    if g + 1 < GROUPS:
-                        x_quantise(g + 1)
-                elif k == "r":
-                    rot_block(g, int(tok[1]))
-                elif k == "v":
-                    value_tile(g, int(tok[1]))
-                elif k == "n":
-                    pass_tile(g, int(tok[1]))
-                elif k == "B":
-                    back_tile(g - 1, int(tok[1]), False)
-        for t in range(T):
-            back_tile(GROUPS - 1, t, True)
+        for g in range(GROUPS + 1):
+            work = g < GROUPS
+            nxt = g + 1 < GROUPS
+            if work:
+                value_tile(g, 0)
+                value_tile(g, 1)
+                rot_block(g, 0)
+                value_finish(g, 0)
+            if nxt:
+                x_transposes(g + 1)
+                x_copy_out(g + 1)
+            if work:
+                value_tile(g, 2)
+                value_tile(g, 3)
+                rot_block(g, 1)
+                value_finish(g, 2)
+            if g == 0:
+                table_part(1)
+            else:
+                back_half(g - 1, 0, 0)
+            if work:
+                pass_tile(g, 0)
+                rot_block(g, 2)
+            if nxt:
+                x_quantise(g + 1)
+            if g == 0:
+                table_part(2)
+            else:
+                back_half(g - 1, 0, 2)
+                back_finish(g - 1, 0)
+            if work:
+                pass_tile(g, 1)
+                rot_block(g, 3)
+                pass_finish(g)
+            if g == 0:
+                table_part(3)
+            else:
+                back_half(g - 1, 2, 0)
+            if work:
+                pass_tile(g, 2)
+                pass_tile(g, 3)
+            if g > 0:
+                back_half(g - 1, 2, 2)
+                back_finish(g - 1, 2)

@@ -222,7 +222,6 @@ def tile_improvedattention_pa_t_kernel(
         oqk = {}
         ovs = {}
         mw = {}
-        bts = {}
 
         def mx(out, lhsT, lhsT_scale, rhs, rhs_scale):
             nc.tensor.matmul_mx(
@@ -288,69 +287,69 @@ def tile_improvedattention_pa_t_kernel(
                 op=ALU.add,
             )
 
-        def back_half(g, t0, i0):
-            if i0 == 0:
-                for t in (t0, t0 + 1):
-                    bts[t] = pst.tile([P, 512], F32, name="bt", tag="t")
-            for i in (i0, i0 + 1):
+        def back_tile(g, t):
+            bt = pst.tile([P, 512], F32, name="bt", tag="t")
+            for i in range(4):
                 for part, moving in ((0, ident_f), (1, perm_f)):
-                    for t in (t0, t0 + 1):
-                        nc.tensor.matmul(
-                            bts[t][:, P * i : P * (i + 1)],
-                            lhsT=mw[(g, i)][:, part, P * t : P * (t + 1)], rhs=moving[:],
-                            is_transpose=True, start=(part == 0), stop=(part == 1),
-                        )
+                    nc.tensor.matmul(
+                        bt[:, P * i : P * (i + 1)],
+                        lhsT=mw[(g, i)][:, part, P * t : P * (t + 1)], rhs=moving[:],
+                        is_transpose=True, start=(part == 0), stop=(part == 1),
+                    )
+            nc.scalar.copy(
+                out=oqk[g][:, :, t, :].rearrange("p q (h d) -> p q h d", d=64)[:, :, :, 0:32],
+                in_=bt[:].rearrange("p (q h j) -> p q h j", q=2, h=8),
+            )
 
-        def back_finish(g, t0):
-            for t in (t0, t0 + 1):
-                nc.scalar.copy(
-                    out=oqk[g][:, :, t, :].rearrange("p q (h d) -> p q h d", d=64)[:, :, :, 0:32],
-                    in_=bts[t][:].rearrange("p (q h j) -> p q h j", q=2, h=8),
-                )
+        def store_qk(g, t0):
             for q in range(2):
                 nc.sync.dma_start(out=out_rows(q, g, t0), in_=oqk[g][:, q, t0 : t0 + 2, :])
 
         for g in range(GROUPS + 1):
             work = g < GROUPS
             nxt = g + 1 < GROUPS
-            if work:
+            if g == 0:
                 value_tile(g, 0)
                 value_tile(g, 1)
                 rot_block(g, 0)
+                rot_block(g, 1)
+            elif work:
+                rot_block(g, 0)
+                rot_block(g, 1)
+                value_tile(g, 0)
+                value_tile(g, 1)
+            if work:
                 value_finish(g, 0)
             if nxt:
                 x_transposes(g + 1)
                 x_copy_out(g + 1)
-            if work:
-                value_tile(g, 2)
-                value_tile(g, 3)
-                rot_block(g, 1)
-                value_finish(g, 2)
             if g == 0:
                 table_part(1)
             else:
-                back_half(g - 1, 0, 0)
+                back_tile(g - 1, 0)
+
             if work:
-                pass_tile(g, 0)
                 rot_block(g, 2)
+                value_tile(g, 2)
+                value_tile(g, 3)
+                value_finish(g, 2)
+                pass_tile(g, 0)
             if nxt:
                 x_quantise(g + 1)
             if g == 0:
                 table_part(2)
-            else:
-                back_half(g - 1, 0, 2)
-                back_finish(g - 1, 0)
-            if work:
-                pass_tile(g, 1)
-                rot_block(g, 3)
-                pass_finish(g)
-            if g == 0:
                 table_part(3)
             else:
-                back_half(g - 1, 2, 0)
+                back_tile(g - 1, 1)
+                store_qk(g - 1, 0)
+                back_tile(g - 1, 2)
+
             if work:
+                rot_block(g, 3)
+                pass_tile(g, 1)
+                pass_finish(g)
                 pass_tile(g, 2)
                 pass_tile(g, 3)
             if g > 0:
-                back_half(g - 1, 2, 2)
-                back_finish(g - 1, 2)
+                back_tile(g - 1, 3)
+                store_qk(g - 1, 2)

@@ -36,8 +36,8 @@ def tile_improvedattention_pa_t_kernel(
         oqkp = ctx.enter_context(tc.tile_pool(name="oqkp", bufs=3))
         ovp = ctx.enter_context(tc.tile_pool(name="ovp", bufs=3))
         psr = ctx.enter_context(tc.psum_pool(name="psr", bufs=2))
-        psa = ctx.enter_context(tc.psum_pool(name="psa", bufs=3))
-        pst = ctx.enter_context(tc.psum_pool(name="pst", bufs=3))
+        psa = ctx.enter_context(tc.psum_pool(name="psa", bufs=6))
+        pst = psa
         ctx.enter_context(nc.allow_non_contiguous_dma(reason="short rows of tables and column chunks"))
         ctx.enter_context(tc.manual_schedule())
 
@@ -71,7 +71,11 @@ def tile_improvedattention_pa_t_kernel(
                     in_=W_qkv[256 * u : 256 * (u + 1), c0 : c0 + 512].rearrange("(q e) c -> q e c", e=2),
                 )
 
-        load_x(0)
+        for hf in range(2):
+            nc.sync.dma_start(
+                out=x_sb[0][:, 1024 * hf : 1024 * (hf + 1)],
+                in_=xf[0:512, :].rearrange("(p t) k -> p t k", t=T)[:, 2 * hf : 2 * hf + 2, :].rearrange("p t k -> p (t k)"),
+            )
         load_w(1024)
         load_w(0)
         load_w(512)
@@ -99,7 +103,7 @@ def tile_improvedattention_pa_t_kernel(
             xw = x_sb[g][:].bitcast(F32)
             banks = []
             for hf in range(2):
-                xt = pst.tile([P, 4, P], F32, name="xt", tag="t")
+                xt = pst.tile([P, 4, P], F32, name="xt", tag="a")
                 for tt in range(2):
                     for u in range(2):
                         c0 = 256 * (2 * hf + tt) + 128 * u
@@ -125,6 +129,8 @@ def tile_improvedattention_pa_t_kernel(
             nc.vector.quantize_mx(out=codes[:].bitcast(FP8X4), scales=scales[:], in_=xgrouped[g][:])
             xc[g] = codes
             xs[g] = scales
+
+        x_transposes(0)
 
         brow = const.tile([P, 1024], BF16, name="brow")
         bqk = bnat[:, 0:1024].rearrange("p (g w j) -> p w g j", g=16, w=2)
@@ -169,7 +175,7 @@ def tile_improvedattention_pa_t_kernel(
         )
 
         def table_part(gp):
-            pt = pst.tile([P, 2, T, P], BF16, name="pt", tag="t")
+            pt = pst.tile([P, 2, T, P], BF16, name="pt", tag="a")
             for tab in range(2):
                 for t in range(T):
                     nc.tensor.transpose(pt[:, tab, t, :], csrep[:, tab, T * gp + t, :], ident_b[:])
@@ -180,7 +186,6 @@ def tile_improvedattention_pa_t_kernel(
         bias_bc = const.tile([P, 1024], F32, name="bias_bc")
         for k in range(2):
             nc.scalar.copy(out=bias_bc[:, 512 * k : 512 * (k + 1)], in_=pbs[k][:])
-        x_transposes(0)
         x_copy_out(0)
         table_part(0)
 
@@ -288,7 +293,7 @@ def tile_improvedattention_pa_t_kernel(
             )
 
         def back_tile(g, t):
-            bt = pst.tile([P, 512], F32, name="bt", tag="t")
+            bt = pst.tile([P, 512], F32, name="bt", tag="a")
             for i in range(4):
                 for part, moving in ((0, ident_f), (1, perm_f)):
                     nc.tensor.matmul(
@@ -305,51 +310,62 @@ def tile_improvedattention_pa_t_kernel(
             for q in range(2):
                 nc.sync.dma_start(out=out_rows(q, g, t0), in_=oqk[g][:, q, t0 : t0 + 2, :])
 
+        def store_qk_tile(g, t):
+            for q in range(2):
+                nc.sync.dma_start(
+                    out=outs[q][512 * g : 512 * (g + 1), :].rearrange("(p t) c -> p t c", t=T)[:, t, :],
+                    in_=oqk[g][:, q, t, :],
+                )
+
         for g in range(GROUPS + 1):
             work = g < GROUPS
             nxt = g + 1 < GROUPS
             if g == 0:
-                value_tile(g, 0)
-                value_tile(g, 1)
+                for t in range(T):
+                    value_tile(g, t)
+                value_finish(g, 0)
+                value_finish(g, 2)
                 rot_block(g, 0)
                 rot_block(g, 1)
             elif work:
                 rot_block(g, 0)
-                rot_block(g, 1)
                 value_tile(g, 0)
                 value_tile(g, 1)
-            if work:
                 value_finish(g, 0)
+                value_tile(g, 2)
+                rot_block(g, 1)
+                value_tile(g, 3)
+                value_finish(g, 2)
             if nxt:
                 x_transposes(g + 1)
                 x_copy_out(g + 1)
             if g == 0:
                 table_part(1)
+                table_part(2)
             else:
                 back_tile(g - 1, 0)
+                back_tile(g - 1, 1)
+                store_qk(g - 1, 0)
 
             if work:
                 rot_block(g, 2)
-                value_tile(g, 2)
-                value_tile(g, 3)
-                value_finish(g, 2)
                 pass_tile(g, 0)
-            if nxt:
-                x_quantise(g + 1)
-            if g == 0:
-                table_part(2)
-                table_part(3)
-            else:
-                back_tile(g - 1, 1)
-                store_qk(g - 1, 0)
-                back_tile(g - 1, 2)
-
-            if work:
-                rot_block(g, 3)
                 pass_tile(g, 1)
                 pass_finish(g)
+            if nxt:
+                x_quantise(g + 1)
+            if work:
+                rot_block(g, 3)
                 pass_tile(g, 2)
                 pass_tile(g, 3)
-            if g > 0:
+            if g == 0:
+                table_part(3)
+            else:
+                back_tile(g - 1, 2)
+                if not work:
+                    store_qk_tile(g - 1, 2)
                 back_tile(g - 1, 3)
-                store_qk(g - 1, 2)
+                if work:
+                    store_qk(g - 1, 2)
+                else:
+                    store_qk_tile(g - 1, 3)

from contextlib import ExitStack

import concourse.mybir as mybir
from concourse.masks import make_identity

F32 = mybir.dt.float32
BF16 = mybir.dt.bfloat16
U32 = mybir.dt.uint32
U8 = mybir.dt.uint8
FP8X4 = mybir.dt.float8_e4m3fn_x4
ALU = mybir.AluOpType

P = 128
TOKENS = 4096
E = 512
GROUPS = 8
T = 4
FLOPS = 2 * TOKENS * E * 3 * E

ROT, PAS, VAL = 0, 512, 1024


def tile_improvedattention_pa_t_kernel(
    tc, x, W_qkv, b_qkv, sin_tab, cos_tab, out_0, out_1, out_2
):
    nc = tc.nc
    xf = x.flatten_outer_dims()
    outs = [o.rearrange("b s h d -> (b s) (h d)") for o in (out_0, out_1, out_2)]

    with ExitStack() as ctx:
        const = ctx.enter_context(tc.tile_pool(name="const", bufs=1))
        xin = ctx.enter_context(tc.tile_pool(name="xin", bufs=GROUPS))
        xgr = ctx.enter_context(tc.tile_pool(name="xgr", bufs=2))
        xq = ctx.enter_context(tc.tile_pool(name="xq", bufs=3))
        mwp = ctx.enter_context(tc.tile_pool(name="mwp", bufs=2))
        oqkp = ctx.enter_context(tc.tile_pool(name="oqkp", bufs=3))
        ovp = ctx.enter_context(tc.tile_pool(name="ovp", bufs=3))
        psr = ctx.enter_context(tc.psum_pool(name="psr", bufs=2))
        psa = ctx.enter_context(tc.psum_pool(name="psa", bufs=6))
        pst = psa
        ctx.enter_context(nc.allow_non_contiguous_dma(reason="short rows of tables and column chunks"))
        ctx.enter_context(tc.manual_schedule())

        bnat = const.tile([P, 3 * E], BF16, name="bnat")
        nc.vector.memset(bnat[:], 0.0)
        ctab = const.tile([P, 16, 32], BF16, name="ctab")
        stab = const.tile([P, 16, 32], BF16, name="stab")
        nc.scalar.dma_start(out=bnat[0:1, :], in_=b_qkv.rearrange("(o c) -> o c", o=1))
        for tab_sb, tab in ((stab, sin_tab), (ctab, cos_tab)):
            nc.scalar.dma_start(
                out=tab_sb[:].rearrange("p (g t) j -> p g (t j)", g=4),
                in_=tab.rearrange("(g p t) j -> p g (t j)", g=4, p=P, t=T),
            )

        x_sb = []
        for g in range(GROUPS):
            x_sb.append(xin.tile([P, T * E], BF16, name="x_sb%d" % g, tag="x_sb"))

        def load_x(g):
            nc.sync.dma_start(
                out=x_sb[g][:],
                in_=xf[512 * g : 512 * (g + 1), :].rearrange("(p t) k -> p (t k)", t=T),
            )

        wraw = const.tile([P, 4, 3 * E], BF16, name="wraw")

        def load_w(c0):
            for u in range(2):
                nc.sync.dma_start(
                    out=wraw[:, 2 * u : 2 * u + 2, c0 : c0 + 512],
                    in_=W_qkv[256 * u : 256 * (u + 1), c0 : c0 + 512].rearrange("(q e) c -> q e c", e=2),
                )

        for hf in range(2):
            nc.sync.dma_start(
                out=x_sb[0][:, 1024 * hf : 1024 * (hf + 1)],
                in_=xf[0:512, :].rearrange("(p t) k -> p t k", t=T)[:, 2 * hf : 2 * hf + 2, :].rearrange("p t k -> p (t k)"),
            )
        load_w(1024)
        load_w(0)
        load_w(512)
        for g in range(1, GROUPS):
            load_x(g)

        ident_f = const.tile([P, P], F32, name="ident_f")
        make_identity(nc, ident_f[:])
        ident_b = const.tile([P, P], BF16, name="ident_b")
        make_identity(nc, ident_b[:])
        ones_b = const.tile([P, P], BF16, name="ones_b")
        nc.vector.memset(ones_b[:], 1.0)
        perm_f = const.tile([P, P], F32, name="perm_f")
        id4 = ident_f[:].rearrange("p (a w i) -> p a w i", a=4, w=2)
        pm4 = perm_f[:].rearrange("p (a w i) -> p a w i", a=4, w=2)
        nc.vector.tensor_copy(out=pm4[:, :, 0, :], in_=id4[:, :, 1, :])
        nc.vector.tensor_copy(out=pm4[:, :, 1, :], in_=id4[:, :, 0, :])

        xc = {}
        xs = {}
        xbanks = {}
        xgrouped = {}

        def x_transposes(g):
            xw = x_sb[g][:].bitcast(F32)
            banks = []
            for hf in range(2):
                xt = pst.tile([P, 4, P], F32, name="xt", tag="a")
                for tt in range(2):
                    for u in range(2):
                        c0 = 256 * (2 * hf + tt) + 128 * u
                        nc.tensor.transpose(xt[:, 2 * tt + u, :], xw[:, c0 : c0 + 128], ident_f[:])
                banks.append(xt)
            xbanks[g] = banks

        def x_copy_out(g):
            grouped = xgr.tile([P, 4 * 512], BF16, name="grouped", tag="grouped", align_bytes=64)
            g32 = grouped[:].bitcast(F32)
            for hf in range(2):
                nc.scalar.copy(
                    out=g32[:, 512 * hf : 512 * (hf + 1)].rearrange(
                        "q (tt p u) -> q tt p u", tt=2, p=P, u=2
                    ),
                    in_=xbanks[g][hf][:].rearrange("q (tt u) p -> q tt p u", tt=2, u=2),
                )
            xgrouped[g] = grouped

        def x_quantise(g):
            codes = xq.tile([P, 512], U32, name="xcodes", tag="xcodes", align_bytes=64)
            scales = xq.tile([P, 512], U8, name="xscales", tag="xscales", align_bytes=64)
            nc.vector.quantize_mx(out=codes[:].bitcast(FP8X4), scales=scales[:], in_=xgrouped[g][:])
            xc[g] = codes
            xs[g] = scales

        x_transposes(0)

        brow = const.tile([P, 1024], BF16, name="brow")
        bqk = bnat[:, 0:1024].rearrange("p (g w j) -> p w g j", g=16, w=2)
        nc.vector.tensor_copy(out=brow[:, 512:1024].rearrange("p (g j) -> p g j", g=16), in_=bqk[:, 1])
        nc.vector.tensor_copy(out=brow[:, 0:512].rearrange("p (g j) -> p g j", g=16), in_=bqk[:, 0])
        pbs = []
        for rhs in (brow[:, 512:1024], bnat[:, 1024:1536]):
            pb = psa.tile([P, 512], F32, name="pb", tag="a")
            nc.tensor.matmul(pb[:], lhsT=ones_b[:], rhs=rhs, start=True, stop=True)
            pbs.append(pb)
        pbt = psa.tile([P, 512], F32, name="pbt", tag="a")
        for i in range(4):
            nc.tensor.matmul(
                pbt[:, 32 * i : 32 * (i + 1)], lhsT=brow[:, P * i : P * (i + 1)], rhs=ones_b[:, 0:32],
                start=True, stop=True,
            )

        csrep = const.tile([P, 2, 16, P], BF16, name="csrep")
        csT = const.tile([P, 2, 2048], BF16, name="csT")
        crep = csrep[:, 0].rearrange("p a (r j) -> p a r j", r=4)
        srep = csrep[:, 1].rearrange("p a (r w i) -> p a r w i", r=4, w=2)

        def spread(tab_part, n, width):
            return tab_part.unsqueeze(2).to_broadcast([P, n, 4, width])

        nc.vector.tensor_copy(out=srep[:, 0:4, :, 0, :], in_=spread(stab[:, 0:4, 16:32], 4, 16))
        nc.vector.tensor_scalar_mul(
            out=srep[:, 0:4, :, 1, :], in0=spread(stab[:, 0:4, 0:16], 4, 16), scalar1=-1.0
        )
        nc.scalar.copy(out=crep[:, 0:4], in_=spread(ctab[:, 0:4, :], 4, 32))
        nc.gpsimd.tensor_scalar(
            out=crep[:, 4:16], in0=spread(ctab[:, 4:16, :], 12, 32),
            scalar1=1.0, scalar2=0.0, op0=ALU.mult, op1=ALU.add,
        )
        nc.gpsimd.tensor_scalar(
            out=srep[:, 4:16, :, 0, :], in0=spread(stab[:, 4:16, 16:32], 12, 16),
            scalar1=1.0, scalar2=0.0, op0=ALU.mult, op1=ALU.add,
        )
        nc.gpsimd.tensor_scalar(
            out=srep[:, 4:16, :, 1, :], in0=spread(stab[:, 4:16, 0:16], 12, 16),
            scalar1=-1.0, scalar2=0.0, op0=ALU.mult, op1=ALU.add,
        )

        def table_part(gp):
            pt = pst.tile([P, 2, T, P], BF16, name="pt", tag="a")
            for tab in range(2):
                for t in range(T):
                    nc.tensor.transpose(pt[:, tab, t, :], csrep[:, tab, T * gp + t, :], ident_b[:])
            nc.scalar.copy(
                out=csT[:, :, 512 * gp : 512 * (gp + 1)], in_=pt[:].rearrange("p b t c -> p b (t c)")
            )

        bias_bc = const.tile([P, 1024], F32, name="bias_bc")
        for k in range(2):
            nc.scalar.copy(out=bias_bc[:, 512 * k : 512 * (k + 1)], in_=pbs[k][:])
        x_copy_out(0)
        table_part(0)

        wg = const.tile([P, 3 * E, 4], BF16, name="wg", align_bytes=64)
        wc = const.tile([P, 3 * E], U32, name="wc", align_bytes=64)
        ws = const.tile([P, 3 * E], U8, name="ws", align_bytes=64)

        def w_quantise(c0):
            nc.vector.quantize_mx(
                out=wc[:, c0 : c0 + 512].bitcast(FP8X4),
                scales=ws[:, c0 : c0 + 512],
                in_=wg[:, c0 : c0 + 512, :].rearrange("q c t -> q (c t)"),
            )

        nc.vector.tensor_copy(
            out=wg[:, VAL : VAL + 512, :].rearrange("q (c i) t -> q c t i", i=4),
            in_=wraw[:, :, 1024:1536].rearrange("q t (c i) -> q c t i", i=4),
        )
        biasT = const.tile([P, 4], F32, name="biasT")
        nc.vector.tensor_copy(
            out=biasT[:], in_=pbt[:, 0:128].rearrange("p (i n) -> p i n", n=32)[:, :, 0]
        )
        w_quantise(VAL)
        x_quantise(0)
        wqk = wraw[:, :, 0:1024].rearrange("q t (g w j) -> q w g j t", g=16, w=2)
        for hf in range(2):
            gs = slice(8 * hf, 8 * (hf + 1))
            nc.vector.tensor_copy(
                out=wg[:, ROT + 256 * hf : ROT + 256 * (hf + 1), :].rearrange("q (g j) t -> q g j t", g=8),
                in_=wqk[:, 0, gs],
            )
            nc.scalar.copy(
                out=wg[:, PAS + 256 * hf : PAS + 256 * (hf + 1), :].rearrange("q (g j) t -> q g j t", g=8),
                in_=wqk[:, 1, gs],
            )
        w_quantise(ROT)
        w_quantise(PAS)

        oqk = {}
        ovs = {}
        mw = {}

        def mx(out, lhsT, lhsT_scale, rhs, rhs_scale):
            nc.tensor.matmul_mx(
                out=out, lhsT=lhsT.bitcast(FP8X4), lhsT_scale=lhsT_scale,
                rhs=rhs.bitcast(FP8X4), rhs_scale=rhs_scale, start=True, stop=True,
            )

        def rot_block(g, i):
            bank = psr.tile([P, 512], F32, name="rbank", tag="r")
            cols = slice(ROT + P * i, ROT + P * (i + 1))
            mx(bank[:], wc[:, cols], ws[:, cols], xc[g][:], xs[g][:])
            m = mwp.tile([P, 2, 512], F32, name="mw%d" % i, tag="mw%d" % i)
            gp = g % 4
            nc.vector.scalar_tensor_tensor(
                out=m[:],
                in0=bank[:].unsqueeze(1).to_broadcast([P, 2, 512]),
                scalar=biasT[:, i : i + 1],
                in1=csT[:, :, 512 * gp : 512 * (gp + 1)],
                op0=ALU.add,
                op1=ALU.mult,
            )
            mw[(g, i)] = m

        def token_bank(g, t, c0):
            bank = psa.tile([P, 512], F32, name="abank", tag="a")
            cols = slice(P * t, P * (t + 1))
            mx(bank[:], xc[g][:, cols], xs[g][:, cols], wc[:, c0 : c0 + 512], ws[:, c0 : c0 + 512])
            return bank

        def out_rows(q, g, t0):
            return outs[q][512 * g : 512 * (g + 1), :].rearrange("(p t) c -> p t c", t=T)[:, t0 : t0 + 2, :]

        def value_tile(g, t):
            if t == 0:
                ovs[g] = ovp.tile([P, T, 512], F32, name="ov", tag="ov")
            bank = token_bank(g, t, VAL)
            nc.scalar.copy(out=ovs[g][:, t, :], in_=bank[:])

        def value_finish(g, t0):
            ov = ovs[g][:, t0 : t0 + 2, :]
            nc.gpsimd.tensor_tensor(
                out=ov, in0=ov, in1=bias_bc[:, 512:1024].unsqueeze(1).to_broadcast([P, 2, 512]), op=ALU.add
            )
            nc.sync.dma_start(out=out_rows(2, g, t0), in_=ov)

        def pass_tile(g, t):
            if t == 0:
                oqk[g] = oqkp.tile([P, 2, T, 512], F32, name="oqk", tag="oqk")
            bank = token_bank(g, t, PAS)
            bv = bank[:].rearrange("p (q h j) -> p q h j", q=2, h=8)
            dst = oqk[g][:, :, t, :].rearrange("p q (h d) -> p q h d", d=64)[:, :, :, 32:64]
            if t >= 2:
                bn = bias_bc[:, 0:512].rearrange("p (q h j) -> p q h j", q=2, h=8)
                nc.vector.tensor_tensor(out=dst, in0=bv, in1=bn, op=ALU.add)
            else:
                nc.scalar.copy(out=dst, in_=bv)

        def pass_finish(g):
            dst = oqk[g][:, :, 0:2, :].rearrange("p q t (h d) -> p q t h d", d=64)[:, :, :, :, 32:64]
            nc.gpsimd.tensor_tensor(
                out=dst, in0=dst,
                in1=bias_bc[:, 0:512].rearrange("p (q o h j) -> p q o h j", q=2, o=1, h=8).to_broadcast([P, 2, 2, 8, 32]),
                op=ALU.add,
            )

        def back_tile(g, t):
            bt = pst.tile([P, 512], F32, name="bt", tag="a")
            for i in range(4):
                for part, moving in ((0, ident_f), (1, perm_f)):
                    nc.tensor.matmul(
                        bt[:, P * i : P * (i + 1)],
                        lhsT=mw[(g, i)][:, part, P * t : P * (t + 1)], rhs=moving[:],
                        is_transpose=True, start=(part == 0), stop=(part == 1),
                    )
            nc.scalar.copy(
                out=oqk[g][:, :, t, :].rearrange("p q (h d) -> p q h d", d=64)[:, :, :, 0:32],
                in_=bt[:].rearrange("p (q h j) -> p q h j", q=2, h=8),
            )

        def store_qk(g, t0):
            for q in range(2):
                nc.sync.dma_start(out=out_rows(q, g, t0), in_=oqk[g][:, q, t0 : t0 + 2, :])

        def store_qk_tile(g, t):
            for q in range(2):
                nc.sync.dma_start(
                    out=outs[q][512 * g : 512 * (g + 1), :].rearrange("(p t) c -> p t c", t=T)[:, t, :],
                    in_=oqk[g][:, q, t, :],
                )

        for g in range(GROUPS + 1):
            work = g < GROUPS
            nxt = g + 1 < GROUPS
            if g == 0:
                for t in range(T):
                    value_tile(g, t)
                value_finish(g, 0)
                value_finish(g, 2)
                rot_block(g, 0)
                rot_block(g, 1)
            elif work:
                rot_block(g, 0)
                value_tile(g, 0)
                value_tile(g, 1)
                value_finish(g, 0)
                value_tile(g, 2)
                rot_block(g, 1)
                value_tile(g, 3)
                value_finish(g, 2)
            if nxt:
                x_transposes(g + 1)
                x_copy_out(g + 1)
            if g == 0:
                table_part(1)
                table_part(2)
            else:
                back_tile(g - 1, 0)
                back_tile(g - 1, 1)
                store_qk(g - 1, 0)

            if work:
                rot_block(g, 2)
                pass_tile(g, 0)
                pass_tile(g, 1)
                pass_finish(g)
            if nxt:
                x_quantise(g + 1)
            if work:
                rot_block(g, 3)
                pass_tile(g, 2)
                pass_tile(g, 3)
            if g == 0:
                table_part(3)
            else:
                back_tile(g - 1, 2)
                if not work:
                    store_qk_tile(g - 1, 2)
                back_tile(g - 1, 3)
                if work:
                    store_qk(g - 1, 2)
                else:
                    store_qk_tile(g - 1, 3)
